import numpy as np
import ml_dtypes


def mxq(x, axis, fmt="e4m3"):
    dtype, down = {"e4m3": (ml_dtypes.float8_e4m3fn, 7), "e5m2": (ml_dtypes.float8_e5m2, 14)}[fmt]
    v = np.moveaxis(np.asarray(x, np.float32).astype(ml_dtypes.bfloat16).astype(np.float64), axis, -1)
    blocks = v.reshape(v.shape[:-1] + (-1, 32))
    amax = np.abs(blocks).max(-1, keepdims=True)
    byte = np.maximum(np.where(amax > 0, np.frexp(amax)[1] - 1 + 127, 0) - down, 1)
    scale = np.exp2(byte - 127.0)
    codes = (blocks / scale).astype(np.float32).astype(dtype).astype(np.float64)
    return np.moveaxis((codes * scale).reshape(v.shape), -1, axis)


WIDE = False


def mx_kscale(k):
    if not WIDE:
        return np.ones(k)
    levels = np.array([10, -10, 5, -5, 0])
    if k % 512:
        return np.exp2(np.random.permutation(np.resize(levels, k // 32))).repeat(32)
    a = np.empty((k // 512, 16))
    for p in range(k // 512):
        a[p, :8] = np.random.permutation(np.resize(levels, 8))
        for g in range(8):
            far = levels[np.abs(levels - a[p, g]) >= 10]
            a[p, g + 8] = far[np.random.randint(len(far))]
    return np.exp2(a.ravel()).repeat(32)


BF16 = ml_dtypes.bfloat16


def bf(x):
    return np.asarray(x, np.float32).astype(BF16)


def f64(x):
    return np.asarray(x).astype(np.float64)


N, C, D, H, W = 2, 8, 512, 4, 4
EPS = 1e-5


def setup_inputs():
    t = np.minimum(mx_kscale(D), 1.0) ** 2
    sig0 = 0.01 * (0.5 + np.random.random_sample((C, D)))
    sig = sig0 * t
    r = np.exp2(np.round(np.log2((sig / np.sqrt(sig**2 + EPS)) / (sig0 / np.sqrt(sig0**2 + EPS)))))
    mu = np.random.standard_normal((C, D))
    z = np.random.standard_normal((N, C, D, H, W))
    x = ((z + mu[None, :, :, None, None]) * sig[None, :, :, None, None]).reshape(N, C * D, H, W)
    weight = (np.eye(D)[None] + np.random.standard_normal((C, D, D)) / np.sqrt(D)) / r[:, None, :]
    return {"x": bf(x), "weight": bf(weight), "bias": bf(np.random.standard_normal(C * D) * 0.3)}


def reference(x, weight, bias):
    x, weight, bias = f64(x), f64(weight), f64(bias)
    n, cd, h, w = x.shape
    c = weight.shape[0]
    d = cd // c
    mean = np.mean(x, axis=(0, 2, 3), keepdims=True)
    var = np.mean(np.square(x - mean), axis=(0, 2, 3), keepdims=True)
    xn = (x - mean) / np.sqrt(var + EPS)
    xg = xn.reshape(n, c, d, h * w)
    out = mxq(weight, 2, "e4m3")[None] @ mxq(xg, 2, "e4m3")
    return out.reshape(n, cd, h, w) + bias[None, :, None, None]

@@ -1,0 +1,260 @@
+from contextlib import ExitStack
+
+import concourse.mybir as mybir
+from concourse.masks import make_identity
+
+F32 = mybir.dt.float32
+BF16 = mybir.dt.bfloat16
+U32 = mybir.dt.uint32
+U8 = mybir.dt.uint8
+I32 = mybir.dt.int32
+FP8X4 = mybir.dt.float8_e4m3fn_x4
+ALU = mybir.AluOpType
+ACT = mybir.ActivationFunctionType
+AXIS = mybir.AxisListType
+
+P = 128
+PACK = 4
+BATCH = 2
+CAPS = 8
+D = 512
+HW = 16
+EPS = 1e-5
+SAMPLES = BATCH * HW
+O_TILES = D // P
+GROUPS = 2
+GROUP_CAPS = CAPS // GROUPS
+GROUP_CH = GROUP_CAPS * PACK
+BANK_TILES = 2
+
+FLOPS = 2 * CAPS * D * D * SAMPLES
+
+
+LAST_TILES = 1
+LAG = 3
+
+
+def centre(nc, pool, x_group):
+    x_by_channel = x_group[:].rearrange("q n c t s -> q (c t) n s")
+    total = pool.tile([P, GROUP_CH], F32)
+    nc.vector.tensor_reduce(out=total[:], in_=x_by_channel, axis=AXIS.XY, op=ALU.add)
+    neg_mean = pool.tile([P, GROUP_CH], F32)
+    nc.vector.tensor_scalar_mul(out=neg_mean[:], in0=total[:], scalar1=-1.0 / SAMPLES)
+    centred = pool.tile([P, GROUP_CH, BATCH, HW], F32)
+    nc.vector.tensor_tensor(
+        out=centred[:],
+        in0=x_by_channel,
+        in1=neg_mean[:].unsqueeze(2).unsqueeze(3).to_broadcast([P, GROUP_CH, BATCH, HW]),
+        op=ALU.add,
+    )
+    return centred
+
+
+def square(nc, pool, centred):
+    squared = pool.tile([P, GROUP_CH, BATCH, HW], F32)
+    nc.scalar.activation(out=squared[:], in_=centred[:], func=ACT.Square)
+    return squared
+
+
+def sum_squares(nc, pool, squared):
+    sum_sq = pool.tile([P, GROUP_CH], F32)
+    nc.vector.tensor_reduce(
+        out=sum_sq[:],
+        in_=squared[:].rearrange("q k n s -> q k (n s)"),
+        axis=AXIS.X,
+        op=ALU.add,
+    )
+    return sum_sq
+
+
+def deviation(nc, pool, sum_sq):
+    var_eps = pool.tile([P, GROUP_CH], F32)
+    nc.vector.tensor_scalar(
+        out=var_eps[:],
+        in0=sum_sq[:],
+        scalar1=1.0 / SAMPLES,
+        scalar2=EPS,
+        op0=ALU.mult,
+        op1=ALU.add,
+    )
+    std = pool.tile([P, GROUP_CH], F32)
+    nc.scalar.activation(out=std[:], in_=var_eps[:], func=ACT.Sqrt)
+    return std
+
+
+def reciprocal(nc, pool, std):
+    rstd = pool.tile([P, GROUP_CH], F32)
+    nc.vector.reciprocal(out=rstd[:], in_=std[:])
+    return rstd
+
+
+def normalise(nc, pool, centred, rstd):
+    xn = pool.tile([P, GROUP_CAPS, SAMPLES, PACK], BF16, align_bytes=64)
+    nc.vector.tensor_tensor(
+        out=xn[:],
+        in0=centred[:].rearrange("q (c t) n s -> q c (n s) t", t=PACK),
+        in1=rstd[:]
+        .rearrange("q (c t) -> q c t", t=PACK)
+        .unsqueeze(2)
+        .to_broadcast([P, GROUP_CAPS, SAMPLES, PACK]),
+        op=ALU.mult,
+    )
+    return xn
+
+
+def quantise_samples(nc, pool, xn):
+    x_codes = pool.tile([P, GROUP_CAPS * SAMPLES], U32, align_bytes=64)
+    x_scales = pool.tile([P, GROUP_CAPS * SAMPLES], U8, align_bytes=64)
+    nc.vector.quantize_mx(
+        out=x_codes[:].bitcast(FP8X4),
+        scales=x_scales[:],
+        in_=xn[:].rearrange("q c m t -> q (c m t)"),
+    )
+    return x_codes, x_scales
+
+
+def turn_weights(nc, pool, turned_pool, w_rows, ident, tiles):
+    w_words = w_rows[:].bitcast(F32)
+    grouped = pool.tile([P, O_TILES, P, PACK], BF16, align_bytes=64)
+    grouped_words = grouped[:].bitcast(F32)
+    for j0 in range(0, O_TILES, tiles):
+        turned = turned_pool.tile([P, tiles, 2, P], F32)
+        for jj in range(tiles):
+            for u in range(2):
+                nc.tensor.transpose(
+                    turned[:, jj, u, :], w_words[:, j0 + jj, u : 2 * P : 2], ident[:]
+                )
+        nc.scalar.copy(
+            out=grouped_words[:, j0 : j0 + tiles],
+            in_=turned[:].rearrange("q j u r -> q j r u"),
+        )
+    return grouped
+
+
+def quantise_weights(nc, pool, grouped, tiles):
+    w_codes = pool.tile([P, O_TILES * P], U32, align_bytes=64)
+    w_scales = pool.tile([P, O_TILES * P], U8, align_bytes=64)
+    for j0 in range(0, O_TILES, tiles):
+        cols = slice(j0 * P, (j0 + tiles) * P)
+        nc.vector.quantize_mx(
+            out=w_codes[:, cols].bitcast(FP8X4),
+            scales=w_scales[:, cols],
+            in_=grouped[:, j0 : j0 + tiles].rearrange("q j r t -> q (j r t)"),
+        )
+    return w_codes, w_scales
+
+
+def multiply(nc, pool, product_pool, w_mx, x_mx, place, bias_c, out_c):
+    w_codes, w_scales = w_mx
+    x_codes, x_scales = x_mx
+    product = product_pool.tile([P, O_TILES, GROUP_CAPS * SAMPLES], F32)
+    for j in range(O_TILES):
+        nc.tensor.matmul_mx(
+            out=product[:, j, :],
+            lhsT=w_codes[:, j * P : (j + 1) * P].bitcast(FP8X4),
+            lhsT_scale=w_scales[:, j * P : (j + 1) * P],
+            rhs=x_codes[:].bitcast(FP8X4),
+            rhs_scale=x_scales[:],
+            start=True,
+            stop=True,
+        )
+    result = pool.tile([P, BATCH, O_TILES, HW], F32)
+    nc.vector.tensor_tensor(
+        out=result[:],
+        in0=product[:, :, place * SAMPLES : (place + 1) * SAMPLES].rearrange(
+            "p j (n s) -> p n j s", n=BATCH
+        ),
+        in1=bias_c.unsqueeze(1).unsqueeze(3).to_broadcast([P, BATCH, O_TILES, HW]),
+        op=ALU.add,
+    )
+    nc.sync.dma_start(out=out_c, in_=result[:].rearrange("p n j s -> p n (j s)"))
+
+
+def tile_caps_bn_s_kernel(tc, x, weight, bias, out):
+    nc = tc.nc
+    with ExitStack() as ctx:
+        consts = ctx.enter_context(tc.tile_pool(name="consts", bufs=1))
+        acts = ctx.enter_context(tc.tile_pool(name="acts", bufs=GROUPS))
+        caps = ctx.enter_context(tc.tile_pool(name="caps", bufs=CAPS))
+        turned_pool = ctx.enter_context(tc.psum_pool(name="turned", bufs=6))
+        product_pool = ctx.enter_context(tc.psum_pool(name="product", bufs=2))
+        ctx.enter_context(tc.manual_schedule())
+
+        x_view = x.rearrange(
+            "n (c q t) h w -> q n c (t h w)", c=CAPS, q=P, t=PACK
+        )
+        x_groups = []
+        for g in range(GROUPS):
+            x_group = acts.tile([P, BATCH, GROUP_CAPS, PACK, HW], BF16)
+            for n in range(BATCH):
+                nc.sync.dma_start(
+                    out=x_group[:, n].rearrange("q c t s -> q c (t s)"),
+                    in_=x_view[:, n, g * GROUP_CAPS : (g + 1) * GROUP_CAPS],
+                )
+            x_groups.append(x_group)
+        w_rows_all = []
+        for c in range(CAPS):
+            w_rows = caps.tile([P, O_TILES, D], BF16)
+            w_view = weight[c].rearrange("(p j) i -> p j i", j=O_TILES)
+            if c < CAPS - 1:
+                nc.sync.dma_start(out=w_rows[:], in_=w_view)
+            else:
+                for j0 in range(0, O_TILES, LAST_TILES):
+                    nc.sync.dma_start(
+                        out=w_rows[:, j0 : j0 + LAST_TILES], in_=w_view[:, j0 : j0 + LAST_TILES]
+                    )
+            w_rows_all.append(w_rows)
+
+        bias_rows = consts.tile([P, D], BF16)
+        nc.vector.memset(bias_rows[:].bitcast(I32), 0)
+        nc.scalar.dma_start(
+            out=bias_rows[0:CAPS, :], in_=bias.rearrange("(c o) -> c o", c=CAPS)
+        )
+        ident = consts.tile([P, P], F32)
+        make_identity(nc, ident[:])
+        ones = consts.tile([P, 1], F32)
+        nc.vector.memset(ones[:], 1.0)
+        table_warmer = consts.tile([P, 1], F32)
+        nc.scalar.activation(out=table_warmer[:], in_=ones[:], func=ACT.Sqrt)
+
+        bias_words = bias_rows[:].bitcast(F32).rearrange("c (p v) -> c v p", v=2)
+        bias_turned = turned_pool.tile([P, 2, P], F32, tag="turned")
+        for v in range(2):
+            nc.tensor.transpose(bias_turned[:, v, :], bias_words[:, v, :], ident[:])
+
+        groups = range(GROUPS)
+        centred = [centre(nc, acts, x_groups[g]) for g in groups]
+        squared = [square(nc, acts, centred[g]) for g in groups]
+        bias_sb = consts.tile([P, CAPS, O_TILES], F32)
+        nc.scalar.copy(
+            out=bias_sb[:].rearrange("p c (v e) -> p c v e", v=2),
+            in_=bias_turned[:].bitcast(BF16).rearrange("p v (c e) -> p c v e", e=2)[:, 0:CAPS],
+        )
+        grouped_0 = turn_weights(nc, caps, turned_pool, w_rows_all[0], ident, BANK_TILES)
+        sum_sq = [sum_squares(nc, acts, squared[g]) for g in groups]
+        std = [deviation(nc, acts, sum_sq[g]) for g in groups]
+        w_mx = [quantise_weights(nc, caps, grouped_0, BANK_TILES)]
+        rstd = [reciprocal(nc, acts, std[g]) for g in groups]
+        xn = [normalise(nc, acts, centred[g], rstd[g]) for g in groups]
+        x_mx = [quantise_samples(nc, acts, xn[g]) for g in groups]
+
+        out_view = out.rearrange(
+            "n (c p j) h w -> c p n (j h w)", c=CAPS, p=P, j=O_TILES
+        )
+        for c in range(1, CAPS + LAG):
+            if c < CAPS:
+                tiles = BANK_TILES if c < CAPS - 1 else LAST_TILES
+                grouped = turn_weights(nc, caps, turned_pool, w_rows_all[c], ident, tiles)
+                w_mx.append(quantise_weights(nc, caps, grouped, tiles))
+            if c >= LAG:
+                m = c - LAG
+                multiply(
+                    nc,
+                    caps,
+                    product_pool,
+                    w_mx[m],
+                    x_mx[m // GROUP_CAPS],
+                    m % GROUP_CAPS,
+                    bias_sb[:, m, :],
+                    out_view[m],
+                )

@@ -22,152 +22,13 @@ HW = 16
 EPS = 1e-5
 SAMPLES = BATCH * HW
 O_TILES = D // P
+PAIR = 2
+PAIRS = CAPS // PAIR
 GROUPS = 2
 GROUP_CAPS = CAPS // GROUPS
 GROUP_CH = GROUP_CAPS * PACK
-BANK_TILES = 2
 
 FLOPS = 2 * CAPS * D * D * SAMPLES
-
-
-LAST_TILES = 1
-LAG = 3
-
-
-def centre(nc, pool, x_group):
-    x_by_channel = x_group[:].rearrange("q n c t s -> q (c t) n s")
-    total = pool.tile([P, GROUP_CH], F32)
-    nc.vector.tensor_reduce(out=total[:], in_=x_by_channel, axis=AXIS.XY, op=ALU.add)
-    neg_mean = pool.tile([P, GROUP_CH], F32)
-    nc.vector.tensor_scalar_mul(out=neg_mean[:], in0=total[:], scalar1=-1.0 / SAMPLES)
-    centred = pool.tile([P, GROUP_CH, BATCH, HW], F32)
-    nc.vector.tensor_tensor(
-        out=centred[:],
-        in0=x_by_channel,
-        in1=neg_mean[:].unsqueeze(2).unsqueeze(3).to_broadcast([P, GROUP_CH, BATCH, HW]),
-        op=ALU.add,
-    )
-    return centred
-
-
-def square(nc, pool, centred):
-    squared = pool.tile([P, GROUP_CH, BATCH, HW], F32)
-    nc.scalar.activation(out=squared[:], in_=centred[:], func=ACT.Square)
-    return squared
-
-
-def sum_squares(nc, pool, squared):
-    sum_sq = pool.tile([P, GROUP_CH], F32)
-    nc.vector.tensor_reduce(
-        out=sum_sq[:],
-        in_=squared[:].rearrange("q k n s -> q k (n s)"),
-        axis=AXIS.X,
-        op=ALU.add,
-    )
-    return sum_sq
-
-
-def deviation(nc, pool, sum_sq):
-    var_eps = pool.tile([P, GROUP_CH], F32)
-    nc.vector.tensor_scalar(
-        out=var_eps[:],
-        in0=sum_sq[:],
-        scalar1=1.0 / SAMPLES,
-        scalar2=EPS,
-        op0=ALU.mult,
-        op1=ALU.add,
-    )
-    std = pool.tile([P, GROUP_CH], F32)
-    nc.scalar.activation(out=std[:], in_=var_eps[:], func=ACT.Sqrt)
-    return std
-
-
-def reciprocal(nc, pool, std):
-    rstd = pool.tile([P, GROUP_CH], F32)
-    nc.vector.reciprocal(out=rstd[:], in_=std[:])
-    return rstd
-
-
-def normalise(nc, pool, centred, rstd):
-    xn = pool.tile([P, GROUP_CAPS, SAMPLES, PACK], BF16, align_bytes=64)
-    nc.vector.tensor_tensor(
-        out=xn[:],
-        in0=centred[:].rearrange("q (c t) n s -> q c (n s) t", t=PACK),
-        in1=rstd[:]
-        .rearrange("q (c t) -> q c t", t=PACK)
-        .unsqueeze(2)
-        .to_broadcast([P, GROUP_CAPS, SAMPLES, PACK]),
-        op=ALU.mult,
-    )
-    return xn
-
-
-def quantise_samples(nc, pool, xn):
-    x_codes = pool.tile([P, GROUP_CAPS * SAMPLES], U32, align_bytes=64)
-    x_scales = pool.tile([P, GROUP_CAPS * SAMPLES], U8, align_bytes=64)
-    nc.vector.quantize_mx(
-        out=x_codes[:].bitcast(FP8X4),
-        scales=x_scales[:],
-        in_=xn[:].rearrange("q c m t -> q (c m t)"),
-    )
-    return x_codes, x_scales
-
-
-def turn_weights(nc, pool, turned_pool, w_rows, ident, tiles):
-    w_words = w_rows[:].bitcast(F32)
-    grouped = pool.tile([P, O_TILES, P, PACK], BF16, align_bytes=64)
-    grouped_words = grouped[:].bitcast(F32)
-    for j0 in range(0, O_TILES, tiles):
-        turned = turned_pool.tile([P, tiles, 2, P], F32)
-        for jj in range(tiles):
-            for u in range(2):
-                nc.tensor.transpose(
-                    turned[:, jj, u, :], w_words[:, j0 + jj, u : 2 * P : 2], ident[:]
-                )
-        nc.scalar.copy(
-            out=grouped_words[:, j0 : j0 + tiles],
-            in_=turned[:].rearrange("q j u r -> q j r u"),
-        )
-    return grouped
-
-
-def quantise_weights(nc, pool, grouped, tiles):
-    w_codes = pool.tile([P, O_TILES * P], U32, align_bytes=64)
-    w_scales = pool.tile([P, O_TILES * P], U8, align_bytes=64)
-    for j0 in range(0, O_TILES, tiles):
-        cols = slice(j0 * P, (j0 + tiles) * P)
-        nc.vector.quantize_mx(
-            out=w_codes[:, cols].bitcast(FP8X4),
-            scales=w_scales[:, cols],
-            in_=grouped[:, j0 : j0 + tiles].rearrange("q j r t -> q (j r t)"),
-        )
-    return w_codes, w_scales
-
-
-def multiply(nc, pool, product_pool, w_mx, x_mx, place, bias_c, out_c):
-    w_codes, w_scales = w_mx
-    x_codes, x_scales = x_mx
-    product = product_pool.tile([P, O_TILES, GROUP_CAPS * SAMPLES], F32)
-    for j in range(O_TILES):
-        nc.tensor.matmul_mx(
-            out=product[:, j, :],
-            lhsT=w_codes[:, j * P : (j + 1) * P].bitcast(FP8X4),
-            lhsT_scale=w_scales[:, j * P : (j + 1) * P],
-            rhs=x_codes[:].bitcast(FP8X4),
-            rhs_scale=x_scales[:],
-            start=True,
-            stop=True,
-        )
-    result = pool.tile([P, BATCH, O_TILES, HW], F32)
-    nc.vector.tensor_tensor(
-        out=result[:],
-        in0=product[:, :, place * SAMPLES : (place + 1) * SAMPLES].rearrange(
-            "p j (n s) -> p n j s", n=BATCH
-        ),
-        in1=bias_c.unsqueeze(1).unsqueeze(3).to_broadcast([P, BATCH, O_TILES, HW]),
-        op=ALU.add,
-    )
-    nc.sync.dma_start(out=out_c, in_=result[:].rearrange("p n j s -> p n (j s)"))
 
 
 def tile_caps_bn_s_kernel(tc, x, weight, bias, out):
@@ -176,34 +37,38 @@ def tile_caps_bn_s_kernel(tc, x, weight, bias, out):
         consts = ctx.enter_context(tc.tile_pool(name="consts", bufs=1))
         acts = ctx.enter_context(tc.tile_pool(name="acts", bufs=GROUPS))
         caps = ctx.enter_context(tc.tile_pool(name="caps", bufs=CAPS))
-        turned_pool = ctx.enter_context(tc.psum_pool(name="turned", bufs=6))
-        product_pool = ctx.enter_context(tc.psum_pool(name="product", bufs=2))
+        banks = ctx.enter_context(tc.psum_pool(name="banks", bufs=8))
         ctx.enter_context(tc.manual_schedule())
 
-        x_view = x.rearrange(
-            "n (c q t) h w -> q n c (t h w)", c=CAPS, q=P, t=PACK
-        )
+        x_view = x.rearrange("n (c q t) h w -> q n c (t h w)", c=CAPS, q=P, t=PACK)
         x_groups = []
-        for g in range(GROUPS):
-            x_group = acts.tile([P, BATCH, GROUP_CAPS, PACK, HW], BF16)
+        w_rows_all = []
+
+        def load_x(g):
+            x_group = acts.tile([P, BATCH, GROUP_CAPS, PACK, HW], BF16, name="x_group")
             for n in range(BATCH):
                 nc.sync.dma_start(
                     out=x_group[:, n].rearrange("q c t s -> q c (t s)"),
                     in_=x_view[:, n, g * GROUP_CAPS : (g + 1) * GROUP_CAPS],
                 )
             x_groups.append(x_group)
-        w_rows_all = []
-        for c in range(CAPS):
-            w_rows = caps.tile([P, O_TILES, D], BF16)
+
+        def load_w(c, j0, tiles):
+            if j0 == 0:
+                w_rows_all.append(caps.tile([P, O_TILES, D], BF16, name="w_rows"))
             w_view = weight[c].rearrange("(p j) i -> p j i", j=O_TILES)
-            if c < CAPS - 1:
-                nc.sync.dma_start(out=w_rows[:], in_=w_view)
-            else:
-                for j0 in range(0, O_TILES, LAST_TILES):
-                    nc.sync.dma_start(
-                        out=w_rows[:, j0 : j0 + LAST_TILES], in_=w_view[:, j0 : j0 + LAST_TILES]
-                    )
-            w_rows_all.append(w_rows)
+            nc.sync.dma_start(
+                out=w_rows_all[c][:, j0 : j0 + tiles], in_=w_view[:, j0 : j0 + tiles]
+            )
+
+        load_w(0, 0, 2)
+        load_x(0)
+        load_x(1)
+        load_w(0, 2, 2)
+        for c in range(1, CAPS - 1):
+            load_w(c, 0, O_TILES)
+        for j in range(O_TILES):
+            load_w(CAPS - 1, j, 1)
 
         bias_rows = consts.tile([P, D], BF16)
         nc.vector.memset(bias_rows[:].bitcast(I32), 0)
@@ -217,44 +82,229 @@ def tile_caps_bn_s_kernel(tc, x, weight, bias, out):
         table_warmer = consts.tile([P, 1], F32)
         nc.scalar.activation(out=table_warmer[:], in_=ones[:], func=ACT.Sqrt)
 
-        bias_words = bias_rows[:].bitcast(F32).rearrange("c (p v) -> c v p", v=2)
-        bias_turned = turned_pool.tile([P, 2, P], F32, tag="turned")
-        for v in range(2):
-            nc.tensor.transpose(bias_turned[:, v, :], bias_words[:, v, :], ident[:])
+        grouped_all = {}
+        turned_all = {}
+        w_codes_all = {}
+        w_scales_all = {}
 
-        groups = range(GROUPS)
-        centred = [centre(nc, acts, x_groups[g]) for g in groups]
-        squared = [square(nc, acts, centred[g]) for g in groups]
-        bias_sb = consts.tile([P, CAPS, O_TILES], F32)
-        nc.scalar.copy(
-            out=bias_sb[:].rearrange("p c (v e) -> p c v e", v=2),
-            in_=bias_turned[:].bitcast(BF16).rearrange("p v (c e) -> p c v e", e=2)[:, 0:CAPS],
-        )
-        grouped_0 = turn_weights(nc, caps, turned_pool, w_rows_all[0], ident, BANK_TILES)
-        sum_sq = [sum_squares(nc, acts, squared[g]) for g in groups]
-        std = [deviation(nc, acts, sum_sq[g]) for g in groups]
-        w_mx = [quantise_weights(nc, caps, grouped_0, BANK_TILES)]
-        rstd = [reciprocal(nc, acts, std[g]) for g in groups]
-        xn = [normalise(nc, acts, centred[g], rstd[g]) for g in groups]
-        x_mx = [quantise_samples(nc, acts, xn[g]) for g in groups]
+        def turn(c, j0, tiles):
+            w_words = w_rows_all[c][:].bitcast(F32)
+            turned = banks.tile([P, tiles, 2, P], F32, name="bank")
+            for jj in range(tiles):
+                for u in range(2):
+                    nc.tensor.transpose(
+                        turned[:, jj, u, :], w_words[:, j0 + jj, u : 2 * P : 2], ident[:]
+                    )
+            turned_all[c, j0] = turned
 
-        out_view = out.rearrange(
-            "n (c p j) h w -> c p n (j h w)", c=CAPS, p=P, j=O_TILES
-        )
-        for c in range(1, CAPS + LAG):
-            if c < CAPS:
-                tiles = BANK_TILES if c < CAPS - 1 else LAST_TILES
-                grouped = turn_weights(nc, caps, turned_pool, w_rows_all[c], ident, tiles)
-                w_mx.append(quantise_weights(nc, caps, grouped, tiles))
-            if c >= LAG:
-                m = c - LAG
-                multiply(
-                    nc,
-                    caps,
-                    product_pool,
-                    w_mx[m],
-                    x_mx[m // GROUP_CAPS],
-                    m % GROUP_CAPS,
-                    bias_sb[:, m, :],
-                    out_view[m],
+        def lift(c, j0, tiles, engine):
+            if c not in grouped_all:
+                grouped_all[c] = caps.tile(
+                    [P, O_TILES, P, PACK], BF16, align_bytes=64, name="grouped"
                 )
+            dst = grouped_all[c][:].bitcast(F32)[:, j0 : j0 + tiles]
+            src = turned_all[c, j0][:].rearrange("q j u r -> q j r u")
+            if engine == "S":
+                nc.scalar.copy(out=dst, in_=src)
+            else:
+                nc.vector.tensor_copy(out=dst, in_=src)
+
+        def quant(c, j0, tiles):
+            if c not in w_codes_all:
+                w_codes_all[c] = caps.tile([P, D], U32, align_bytes=64, name="w_codes")
+                w_scales_all[c] = caps.tile([P, D], U8, align_bytes=64, name="w_scales")
+            cols = slice(j0 * P, (j0 + tiles) * P)
+            nc.vector.quantize_mx(
+                out=w_codes_all[c][:, cols].bitcast(FP8X4),
+                scales=w_scales_all[c][:, cols],
+                in_=grouped_all[c][:, j0 : j0 + tiles].rearrange("q j r t -> q (j r t)"),
+            )
+
+        stats = consts.tile([P, CAPS * PACK // 2, 2, 3], F32)
+        stat_of = stats[:].rearrange("q k e m -> q (k e) m")
+        var_eps = consts.tile([P, GROUPS * GROUP_CH], F32)
+        std = consts.tile([P, GROUPS * GROUP_CH], F32)
+        rstd = consts.tile([P, GROUPS * GROUP_CH], F32)
+        centred = []
+        xn = consts.tile([P, CAPS, SAMPLES, PACK], BF16, align_bytes=64)
+        x_codes = consts.tile([P, CAPS * SAMPLES], U32, align_bytes=64)
+        x_scales = consts.tile([P, CAPS * SAMPLES], U8, align_bytes=64)
+
+        def chans(g):
+            return slice(g * GROUP_CH, (g + 1) * GROUP_CH)
+
+        def by_channel(g):
+            return x_groups[g][:].rearrange("q n c t s -> q (c t) n s")
+
+        def bn(g):
+            for k in range(g * GROUP_CH // 2, (g + 1) * GROUP_CH // 2):
+                c, e = divmod(k - g * GROUP_CH // 2, PACK // 2)
+                nc.vector.bn_stats(
+                    out=stats[:, k].rearrange("q e m -> q (e m)"),
+                    in_=x_groups[g][:, :, c, 2 * e : 2 * e + 2, :].rearrange("q n t s -> q n s t"),
+                )
+
+        def centre(g, engine):
+            t = acts.tile([P, GROUP_CH, BATCH, HW], F32, name="centred")
+            engine.tensor_tensor(
+                out=t[:],
+                in0=by_channel(g),
+                in1=stat_of[:, chans(g), 1]
+                .unsqueeze(2)
+                .unsqueeze(3)
+                .to_broadcast([P, GROUP_CH, BATCH, HW]),
+                op=ALU.subtract,
+            )
+            centred.append(t)
+
+        def of(gs):
+            return slice(gs[0] * GROUP_CH, (gs[-1] + 1) * GROUP_CH)
+
+        def variances(gs=(0, 1)):
+            nc.vector.tensor_scalar(
+                out=var_eps[:, of(gs)],
+                in0=stat_of[:, of(gs), 2],
+                scalar1=1.0 / SAMPLES,
+                scalar2=EPS,
+                op0=ALU.mult,
+                op1=ALU.add,
+            )
+
+        def roots(gs=(0, 1)):
+            nc.scalar.activation(out=std[:, of(gs)], in_=var_eps[:, of(gs)], func=ACT.Sqrt)
+
+        def reciprocals(gs=(0, 1)):
+            nc.vector.reciprocal(out=rstd[:, of(gs)], in_=std[:, of(gs)])
+
+        def normalise(g, engine):
+            engine.tensor_tensor(
+                out=xn[:, g * GROUP_CAPS : (g + 1) * GROUP_CAPS],
+                in0=centred[g][:].rearrange("q (c t) n s -> q c (n s) t", t=PACK),
+                in1=rstd[:, chans(g)]
+                .rearrange("q (c t) -> q c t", t=PACK)
+                .unsqueeze(2)
+                .to_broadcast([P, GROUP_CAPS, SAMPLES, PACK]),
+                op=ALU.mult,
+            )
+
+        def quantise_x(gs=(0, 1)):
+            c0, c1 = gs[0] * GROUP_CAPS, (gs[-1] + 1) * GROUP_CAPS
+            cols = slice(c0 * SAMPLES, c1 * SAMPLES)
+            nc.vector.quantize_mx(
+                out=x_codes[:, cols].bitcast(FP8X4),
+                scales=x_scales[:, cols],
+                in_=xn[:, c0:c1].rearrange("q c m t -> q (c m t)"),
+            )
+
+        out_view = out.rearrange("n (c p j) h w -> p c n (j h w)", c=CAPS, p=P, j=O_TILES)
+        products = {}
+
+        def multiply(c, own=False):
+            h = c // PAIR
+            if c % PAIR == 0 or own:
+                products[c] = banks.tile([P, PAIR, O_TILES, PAIR * SAMPLES], F32, name="bank")
+            else:
+                products[c] = products[c - 1]
+            cols = slice(h * PAIR * SAMPLES, (h + 1) * PAIR * SAMPLES)
+            for j in range(O_TILES):
+                nc.tensor.matmul_mx(
+                    out=products[c][:, c % PAIR, j, :],
+                    lhsT=w_codes_all[c][:, j * P : (j + 1) * P].bitcast(FP8X4),
+                    lhsT_scale=w_scales_all[c][:, j * P : (j + 1) * P],
+                    rhs=x_codes[:, cols].bitcast(FP8X4),
+                    rhs_scale=x_scales[:, cols],
+                    start=True,
+                    stop=True,
+                )
+
+        def finish(c):
+            k = c % PAIR
+            result = caps.tile([P, BATCH, O_TILES, HW], F32, name="result")
+            nc.vector.tensor_tensor(
+                out=result[:],
+                in0=products[c][:, k, :, k * SAMPLES : (k + 1) * SAMPLES].rearrange(
+                    "p j (n s) -> p n j s", n=BATCH
+                ),
+                in1=bias_sb[:, c, :].unsqueeze(1).unsqueeze(3).to_broadcast(
+                    [P, BATCH, O_TILES, HW]
+                ),
+                op=ALU.add,
+            )
+            nc.sync.dma_start(
+                out=out_view[:, c], in_=result[:].rearrange("p n j s -> p n (j s)")
+            )
+
+        def bias_turn():
+            bias_words = bias_rows[:].bitcast(F32).rearrange("c (p v) -> c v p", v=2)
+            bias_turned = banks.tile([P, 2, P], F32, name="bank")
+            for v in range(2):
+                nc.tensor.transpose(bias_turned[:, v, :], bias_words[:, v, :], ident[:])
+            turned_all["bias"] = bias_turned
+
+        bias_sb = consts.tile([P, CAPS, O_TILES], F32)
+
+        def biascopy():
+            nc.scalar.copy(
+                out=bias_sb[:].rearrange("p c (v e) -> p c v e", v=2),
+                in_=turned_all["bias"][:].bitcast(BF16).rearrange(
+                    "p v (c e) -> p c v e", e=2
+                )[:, 0:CAPS],
+            )
+
+        turn(0,0,2)
+        lift(0,0,2, "S")
+        bn(0)
+        variances([0])
+        centre(0, nc.vector)
+        turn(0,2,2)
+        bias_turn()
+        lift(0,2,2, "S")
+        roots([0])
+        biascopy()
+        bn(1)
+        variances([1])
+        centre(1, nc.vector)
+        reciprocals([0])
+        normalise(0, nc.vector)
+        turn(1,0,2); turn(1,2,2)
+        lift(1,0,2, "S")
+        roots([1])
+        lift(1,2,2, "S")
+        quant(0,0,4)
+        quantise_x([0])
+        reciprocals([1])
+        normalise(1, nc.vector)
+        turn(2,0,2); turn(2,2,2)
+        lift(2,0,2, "S"); lift(2,2,2, "S")
+        quant(1,0,4)
+        quantise_x([1])
+        turn(3,0,2); turn(3,2,2)
+        lift(3,0,2, "S"); lift(3,2,2, "S")
+        quant(2,0,4)
+        turn(4,0,2); turn(4,2,2)
+        lift(4,0,2, "S"); lift(4,2,2, "S")
+        quant(3,0,4)
+        multiply(0); multiply(1)
+        turn(5,0,2); turn(5,2,2)
+        finish(0); finish(1)
+        lift(5,0,2, "S"); lift(5,2,2, "S")
+        quant(4,0,4)
+        turn(6,0,2); turn(6,2,2)
+        multiply(2); multiply(3)
+        lift(6,0,2, "S"); lift(6,2,2, "S")
+        quant(5,0,4)
+        finish(2); finish(3)
+        turn(7,0,1); turn(7,1,1); turn(7,2,1); turn(7,3,1)
+        multiply(4); multiply(5)
+        lift(7,0,1, "S")
+        quant(6,0,4)
+        lift(7,1,1, "S")
+        lift(7,2,1, "V")
+        lift(7,3,1, "S")
+        quant(7,0,2)
+        multiply(6,True)
+        quant(7,2,2)
+        finish(4); finish(5)
+        multiply(7,True)
+        finish(6)
+        finish(7)

@@ -63,12 +63,22 @@ def tile_caps_bn_s_kernel(tc, x, weight, bias, out):
 
         load_w(0, 0, 2)
         load_x(0)
-        load_x(1)
         load_w(0, 2, 2)
-        for c in range(1, CAPS - 1):
-            load_w(c, 0, O_TILES)
-        for j in range(O_TILES):
-            load_w(CAPS - 1, j, 1)
+        load_x(1)
+        load_w(1, 0, O_TILES)
+        load_w(2, 0, O_TILES)
+        load_w(3, 0, 2)
+        load_w(3, 2, 2)
+        load_w(4, 0, 2)
+        load_w(4, 2, 2)
+        load_w(5, 0, 2)
+        load_w(5, 2, 2)
+        load_w(6, 0, 2)
+        load_w(6, 2, 2)
+        load_w(7, 0, 1)
+        load_w(7, 1, 1)
+        load_w(7, 2, 1)
+        load_w(7, 3, 1)
 
         bias_rows = consts.tile([P, D], BF16)
         nc.vector.memset(bias_rows[:].bitcast(I32), 0)
@@ -80,7 +90,9 @@ def tile_caps_bn_s_kernel(tc, x, weight, bias, out):
         ones = consts.tile([P, 1], F32)
         nc.vector.memset(ones[:], 1.0)
         table_warmer = consts.tile([P, 1], F32)
-        nc.scalar.activation(out=table_warmer[:], in_=ones[:], func=ACT.Sqrt)
+        nc.scalar.activation(out=table_warmer[:], in_=ones[:], func=ACT.Abs_reciprocal_sqrt)
+        eps = consts.tile([P, 1], F32)
+        nc.vector.tensor_scalar_mul(out=eps[:], in0=ones[:], scalar1=EPS)
 
         grouped_all = {}
         turned_all = {}
@@ -122,8 +134,6 @@ def tile_caps_bn_s_kernel(tc, x, weight, bias, out):
 
         stats = consts.tile([P, CAPS * PACK // 2, 2, 3], F32)
         stat_of = stats[:].rearrange("q k e m -> q (k e) m")
-        var_eps = consts.tile([P, GROUPS * GROUP_CH], F32)
-        std = consts.tile([P, GROUPS * GROUP_CH], F32)
         rstd = consts.tile([P, GROUPS * GROUP_CH], F32)
         centred = []
         xn = consts.tile([P, CAPS, SAMPLES, PACK], BF16, align_bytes=64)
@@ -160,21 +170,14 @@ def tile_caps_bn_s_kernel(tc, x, weight, bias, out):
         def of(gs):
             return slice(gs[0] * GROUP_CH, (gs[-1] + 1) * GROUP_CH)
 
-        def variances(gs=(0, 1)):
-            nc.vector.tensor_scalar(
-                out=var_eps[:, of(gs)],
-                in0=stat_of[:, of(gs), 2],
-                scalar1=1.0 / SAMPLES,
-                scalar2=EPS,
-                op0=ALU.mult,
-                op1=ALU.add,
-            )
-
         def roots(gs=(0, 1)):
-            nc.scalar.activation(out=std[:, of(gs)], in_=var_eps[:, of(gs)], func=ACT.Sqrt)
-
-        def reciprocals(gs=(0, 1)):
-            nc.vector.reciprocal(out=rstd[:, of(gs)], in_=std[:, of(gs)])
+            nc.scalar.activation(
+                out=rstd[:, of(gs)],
+                in_=stat_of[:, of(gs), 2],
+                func=ACT.Abs_reciprocal_sqrt,
+                scale=1.0 / SAMPLES,
+                bias=eps[:],
+            )
 
         def normalise(g, engine):
             engine.tensor_tensor(
@@ -199,16 +202,20 @@ def tile_caps_bn_s_kernel(tc, x, weight, bias, out):
         out_view = out.rearrange("n (c p j) h w -> p c n (j h w)", c=CAPS, p=P, j=O_TILES)
         products = {}
 
+        def start(c, j):
+            k = c % PAIR
+            return (k * O_TILES + j) * PAIR * SAMPLES - k * SAMPLES
+
         def multiply(c, own=False):
             h = c // PAIR
             if c % PAIR == 0 or own:
-                products[c] = banks.tile([P, PAIR, O_TILES, PAIR * SAMPLES], F32, name="bank")
+                products[c] = banks.tile([P, PAIR * O_TILES * PAIR * SAMPLES], F32, name="bank")
             else:
                 products[c] = products[c - 1]
             cols = slice(h * PAIR * SAMPLES, (h + 1) * PAIR * SAMPLES)
             for j in range(O_TILES):
                 nc.tensor.matmul_mx(
-                    out=products[c][:, c % PAIR, j, :],
+                    out=products[c][:, start(c, j) : start(c, j) + PAIR * SAMPLES],
                     lhsT=w_codes_all[c][:, j * P : (j + 1) * P].bitcast(FP8X4),
                     lhsT_scale=w_scales_all[c][:, j * P : (j + 1) * P],
                     rhs=x_codes[:, cols].bitcast(FP8X4),
@@ -218,13 +225,14 @@ def tile_caps_bn_s_kernel(tc, x, weight, bias, out):
                 )
 
         def finish(c):
-            k = c % PAIR
+            b0 = c % PAIR * O_TILES
             result = caps.tile([P, BATCH, O_TILES, HW], F32, name="result")
             nc.vector.tensor_tensor(
                 out=result[:],
-                in0=products[c][:, k, :, k * SAMPLES : (k + 1) * SAMPLES].rearrange(
-                    "p j (n s) -> p n j s", n=BATCH
-                ),
+                in0=products[c][:]
+                .rearrange("p (b k n s) -> p n b k s", k=PAIR, n=BATCH, s=HW)[
+                    :, :, b0 : b0 + O_TILES, 0
+                ],
                 in1=bias_sb[:, c, :].unsqueeze(1).unsqueeze(3).to_broadcast(
                     [P, BATCH, O_TILES, HW]
                 ),
@@ -233,6 +241,28 @@ def tile_caps_bn_s_kernel(tc, x, weight, bias, out):
             nc.sync.dma_start(
                 out=out_view[:, c], in_=result[:].rearrange("p n j s -> p n (j s)")
             )
+
+        def finish2(c):
+            result = caps.tile([P, BATCH, PAIR * O_TILES, HW], F32, name="result2")
+            nc.vector.tensor_tensor(
+                out=result[:],
+                in0=products[c][:].rearrange(
+                    "p (b k n s) -> p n b k s", k=PAIR, n=BATCH, s=HW
+                )[:, :, :, 0],
+                in1=bias_sb[:, c : c + PAIR, :]
+                .rearrange("p k j -> p (k j)")
+                .unsqueeze(1)
+                .unsqueeze(3)
+                .to_broadcast([P, BATCH, PAIR * O_TILES, HW]),
+                op=ALU.add,
+            )
+            for n in range(BATCH):
+                nc.sync.dma_start(
+                    out=out_view2[:, n, c : c + PAIR],
+                    in_=result[:, n].rearrange("p (k j) s -> p k (j s)", k=PAIR),
+                )
+
+        out_view2 = out.rearrange("n (c p j) h w -> p n c (j h w)", c=CAPS, p=P, j=O_TILES)
 
         def bias_turn():
             bias_words = bias_rows[:].bitcast(F32).rearrange("c (p v) -> c v p", v=2)
@@ -254,57 +284,57 @@ def tile_caps_bn_s_kernel(tc, x, weight, bias, out):
         turn(0,0,2)
         lift(0,0,2, "S")
         bn(0)
-        variances([0])
         centre(0, nc.vector)
+        bn(1)
+        centre(1, nc.vector)
         turn(0,2,2)
         bias_turn()
         lift(0,2,2, "S")
-        roots([0])
+        roots()
         biascopy()
-        bn(1)
-        variances([1])
-        centre(1, nc.vector)
-        reciprocals([0])
+        quant(0,0,4)
         normalise(0, nc.vector)
+        normalise(1, nc.vector)
         turn(1,0,2); turn(1,2,2)
         lift(1,0,2, "S")
-        roots([1])
         lift(1,2,2, "S")
-        quant(0,0,4)
-        quantise_x([0])
-        reciprocals([1])
-        normalise(1, nc.vector)
+        quantise_x()
         turn(2,0,2); turn(2,2,2)
-        lift(2,0,2, "S"); lift(2,2,2, "S")
+        lift(2,0,2, "S")
         quant(1,0,4)
-        quantise_x([1])
+        lift(2,2,2, "S")
         turn(3,0,2); turn(3,2,2)
-        lift(3,0,2, "S"); lift(3,2,2, "S")
+        lift(3,0,2, "S")
         quant(2,0,4)
+        lift(3,2,2, "S")
         turn(4,0,2); turn(4,2,2)
-        lift(4,0,2, "S"); lift(4,2,2, "S")
+        lift(4,0,2, "S")
         quant(3,0,4)
-        multiply(0); multiply(1)
+        lift(4,2,2, "S")
         turn(5,0,2); turn(5,2,2)
-        finish(0); finish(1)
-        lift(5,0,2, "S"); lift(5,2,2, "S")
+        lift(5,0,2, "V")
         quant(4,0,4)
+        lift(5,2,2, "S")
         turn(6,0,2); turn(6,2,2)
-        multiply(2); multiply(3)
-        lift(6,0,2, "S"); lift(6,2,2, "S")
+        lift(6,0,2, "S")
         quant(5,0,4)
-        finish(2); finish(3)
-        turn(7,0,1); turn(7,1,1); turn(7,2,1); turn(7,3,1)
+        lift(6,2,2, "S")
+        turn(7,0,1); turn(7,1,1)
+        turn(7,2,1); turn(7,3,1)
+        multiply(0); multiply(1)
+        multiply(2); multiply(3)
         multiply(4); multiply(5)
         lift(7,0,1, "S")
         quant(6,0,4)
         lift(7,1,1, "S")
-        lift(7,2,1, "V")
+        lift(7,2,1, "S")
         lift(7,3,1, "S")
         quant(7,0,2)
         multiply(6,True)
+        finish2(0)
+        finish2(2)
         quant(7,2,2)
-        finish(4); finish(5)
         multiply(7,True)
+        finish2(4)
         finish(6)
         finish(7)

@@ -61,16 +61,14 @@ def tile_caps_bn_s_kernel(tc, x, weight, bias, out):
                 out=w_rows_all[c][:, j0 : j0 + tiles], in_=w_view[:, j0 : j0 + tiles]
             )
 
-        load_w(0, 0, 2)
         load_x(0)
+        load_w(0, 0, 2)
         load_w(0, 2, 2)
-        load_x(1)
         load_w(1, 0, O_TILES)
         load_w(2, 0, O_TILES)
-        load_w(3, 0, 2)
-        load_w(3, 2, 2)
-        load_w(4, 0, 2)
-        load_w(4, 2, 2)
+        load_w(3, 0, O_TILES)
+        load_x(1)
+        load_w(4, 0, O_TILES)
         load_w(5, 0, 2)
         load_w(5, 2, 2)
         load_w(6, 0, 2)
@@ -202,20 +200,13 @@ def tile_caps_bn_s_kernel(tc, x, weight, bias, out):
         out_view = out.rearrange("n (c p j) h w -> p c n (j h w)", c=CAPS, p=P, j=O_TILES)
         products = {}
 
-        def start(c, j):
-            k = c % PAIR
-            return (k * O_TILES + j) * PAIR * SAMPLES - k * SAMPLES
-
-        def multiply(c, own=False):
-            h = c // PAIR
-            if c % PAIR == 0 or own:
-                products[c] = banks.tile([P, PAIR * O_TILES * PAIR * SAMPLES], F32, name="bank")
-            else:
-                products[c] = products[c - 1]
-            cols = slice(h * PAIR * SAMPLES, (h + 1) * PAIR * SAMPLES)
+        def multiply(c):
+            h = c // GROUP_CAPS
+            products[c] = banks.tile([P, O_TILES, GROUP_CAPS * SAMPLES], F32, name="bank")
+            cols = slice(h * GROUP_CAPS * SAMPLES, (h + 1) * GROUP_CAPS * SAMPLES)
             for j in range(O_TILES):
                 nc.tensor.matmul_mx(
-                    out=products[c][:, start(c, j) : start(c, j) + PAIR * SAMPLES],
+                    out=products[c][:, j, :],
                     lhsT=w_codes_all[c][:, j * P : (j + 1) * P].bitcast(FP8X4),
                     lhsT_scale=w_scales_all[c][:, j * P : (j + 1) * P],
                     rhs=x_codes[:, cols].bitcast(FP8X4),
@@ -225,14 +216,13 @@ def tile_caps_bn_s_kernel(tc, x, weight, bias, out):
                 )
 
         def finish(c):
-            b0 = c % PAIR * O_TILES
+            k = c % GROUP_CAPS
             result = caps.tile([P, BATCH, O_TILES, HW], F32, name="result")
             nc.vector.tensor_tensor(
                 out=result[:],
-                in0=products[c][:]
-                .rearrange("p (b k n s) -> p n b k s", k=PAIR, n=BATCH, s=HW)[
-                    :, :, b0 : b0 + O_TILES, 0
-                ],
+                in0=products[c][:, :, k * SAMPLES : (k + 1) * SAMPLES].rearrange(
+                    "p j (n s) -> p n j s", n=BATCH
+                ),
                 in1=bias_sb[:, c, :].unsqueeze(1).unsqueeze(3).to_broadcast(
                     [P, BATCH, O_TILES, HW]
                 ),
@@ -241,28 +231,6 @@ def tile_caps_bn_s_kernel(tc, x, weight, bias, out):
             nc.sync.dma_start(
                 out=out_view[:, c], in_=result[:].rearrange("p n j s -> p n (j s)")
             )
-
-        def finish2(c):
-            result = caps.tile([P, BATCH, PAIR * O_TILES, HW], F32, name="result2")
-            nc.vector.tensor_tensor(
-                out=result[:],
-                in0=products[c][:].rearrange(
-                    "p (b k n s) -> p n b k s", k=PAIR, n=BATCH, s=HW
-                )[:, :, :, 0],
-                in1=bias_sb[:, c : c + PAIR, :]
-                .rearrange("p k j -> p (k j)")
-                .unsqueeze(1)
-                .unsqueeze(3)
-                .to_broadcast([P, BATCH, PAIR * O_TILES, HW]),
-                op=ALU.add,
-            )
-            for n in range(BATCH):
-                nc.sync.dma_start(
-                    out=out_view2[:, n, c : c + PAIR],
-                    in_=result[:, n].rearrange("p (k j) s -> p k (j s)", k=PAIR),
-                )
-
-        out_view2 = out.rearrange("n (c p j) h w -> p n c (j h w)", c=CAPS, p=P, j=O_TILES)
 
         def bias_turn():
             bias_words = bias_rows[:].bitcast(F32).rearrange("c (p v) -> c v p", v=2)
@@ -281,60 +249,68 @@ def tile_caps_bn_s_kernel(tc, x, weight, bias, out):
                 )[:, 0:CAPS],
             )
 
-        turn(0,0,2)
-        lift(0,0,2, "S")
         bn(0)
         centre(0, nc.vector)
-        bn(1)
-        centre(1, nc.vector)
+        turn(0,0,2)
+        lift(0,0,2, "S")
         turn(0,2,2)
-        bias_turn()
+        roots([0])
         lift(0,2,2, "S")
-        roots()
-        biascopy()
-        quant(0,0,4)
         normalise(0, nc.vector)
-        normalise(1, nc.vector)
         turn(1,0,2); turn(1,2,2)
+        bias_turn()
+        quantise_x([0])
         lift(1,0,2, "S")
+        quant(0,0,4)
         lift(1,2,2, "S")
-        quantise_x()
+        biascopy()
         turn(2,0,2); turn(2,2,2)
-        lift(2,0,2, "S")
         quant(1,0,4)
+        lift(2,0,2, "S")
         lift(2,2,2, "S")
         turn(3,0,2); turn(3,2,2)
-        lift(3,0,2, "S")
         quant(2,0,4)
+        multiply(0)
+        multiply(1)
+        lift(3,0,2, "S")
         lift(3,2,2, "S")
         turn(4,0,2); turn(4,2,2)
-        lift(4,0,2, "S")
+        bn(1)
+        centre(1, nc.vector)
         quant(3,0,4)
+        lift(4,0,2, "S")
+        roots([1])
         lift(4,2,2, "S")
+        normalise(1, nc.vector)
+        finish(0)
+        finish(1)
         turn(5,0,2); turn(5,2,2)
-        lift(5,0,2, "V")
         quant(4,0,4)
+        multiply(2)
+        multiply(3)
+        lift(5,0,2, "S")
         lift(5,2,2, "S")
+        quantise_x([1])
         turn(6,0,2); turn(6,2,2)
-        lift(6,0,2, "S")
         quant(5,0,4)
+        lift(6,0,2, "S")
         lift(6,2,2, "S")
+        finish(2)
+        finish(3)
         turn(7,0,1); turn(7,1,1)
         turn(7,2,1); turn(7,3,1)
-        multiply(0); multiply(1)
-        multiply(2); multiply(3)
-        multiply(4); multiply(5)
-        lift(7,0,1, "S")
         quant(6,0,4)
+        multiply(4)
+        multiply(5)
+        multiply(6)
+        lift(7,0,1, "S")
         lift(7,1,1, "S")
+        quant(7,0,2)
         lift(7,2,1, "S")
         lift(7,3,1, "S")
-        quant(7,0,2)
-        multiply(6,True)
-        finish2(0)
-        finish2(2)
+        finish(4)
         quant(7,2,2)
-        multiply(7,True)
-        finish2(4)
+        multiply(7)
+        finish(5)
         finish(6)
         finish(7)

@@ -40,6 +40,8 @@ def tile_caps_bn_s_kernel(tc, x, weight, bias, out):
         banks = ctx.enter_context(tc.psum_pool(name="banks", bufs=8))
         ctx.enter_context(tc.manual_schedule())
 
+        bias_rows = consts.tile([P, D], BF16)
+        nc.vector.memset(bias_rows[:].bitcast(I32), 0)
         x_view = x.rearrange("n (c q t) h w -> q n c (t h w)", c=CAPS, q=P, t=PACK)
         x_groups = []
         w_rows_all = []
@@ -53,6 +55,11 @@ def tile_caps_bn_s_kernel(tc, x, weight, bias, out):
                 )
             x_groups.append(x_group)
 
+        def load_bias():
+            nc.sync.dma_start(
+                out=bias_rows[0:CAPS, :], in_=bias.rearrange("(c o) -> c o", c=CAPS)
+            )
+
         def load_w(c, j0, tiles):
             if j0 == 0:
                 w_rows_all.append(caps.tile([P, O_TILES, D], BF16, name="w_rows"))
@@ -64,11 +71,16 @@ def tile_caps_bn_s_kernel(tc, x, weight, bias, out):
         load_x(0)
         load_w(0, 0, 2)
         load_w(0, 2, 2)
-        load_w(1, 0, O_TILES)
-        load_w(2, 0, O_TILES)
-        load_w(3, 0, O_TILES)
+        load_w(1, 0, 2)
+        load_w(1, 2, 2)
+        load_w(2, 0, 2)
+        load_w(2, 2, 2)
+        load_bias()
+        load_w(3, 0, 2)
+        load_w(3, 2, 2)
         load_x(1)
-        load_w(4, 0, O_TILES)
+        load_w(4, 0, 2)
+        load_w(4, 2, 2)
         load_w(5, 0, 2)
         load_w(5, 2, 2)
         load_w(6, 0, 2)
@@ -78,11 +90,6 @@ def tile_caps_bn_s_kernel(tc, x, weight, bias, out):
         load_w(7, 2, 1)
         load_w(7, 3, 1)
 
-        bias_rows = consts.tile([P, D], BF16)
-        nc.vector.memset(bias_rows[:].bitcast(I32), 0)
-        nc.scalar.dma_start(
-            out=bias_rows[0:CAPS, :], in_=bias.rearrange("(c o) -> c o", c=CAPS)
-        )
         ident = consts.tile([P, P], F32)
         make_identity(nc, ident[:])
         ones = consts.tile([P, 1], F32)
@@ -252,45 +259,45 @@ def tile_caps_bn_s_kernel(tc, x, weight, bias, out):
         bn(0)
         centre(0, nc.vector)
         turn(0,0,2)
+        roots([0])
         lift(0,0,2, "S")
         turn(0,2,2)
-        roots([0])
         lift(0,2,2, "S")
         normalise(0, nc.vector)
         turn(1,0,2); turn(1,2,2)
-        bias_turn()
         quantise_x([0])
         lift(1,0,2, "S")
         quant(0,0,4)
         lift(1,2,2, "S")
-        biascopy()
         turn(2,0,2); turn(2,2,2)
         quant(1,0,4)
         lift(2,0,2, "S")
         lift(2,2,2, "S")
         turn(3,0,2); turn(3,2,2)
+        bn(1)
+        centre(1, nc.vector)
         quant(2,0,4)
+        bias_turn()
         multiply(0)
         multiply(1)
         lift(3,0,2, "S")
+        roots([1])
         lift(3,2,2, "S")
+        biascopy()
+        normalise(1, nc.vector)
         turn(4,0,2); turn(4,2,2)
-        bn(1)
-        centre(1, nc.vector)
         quant(3,0,4)
         lift(4,0,2, "S")
-        roots([1])
         lift(4,2,2, "S")
-        normalise(1, nc.vector)
         finish(0)
         finish(1)
+        quantise_x([1])
         turn(5,0,2); turn(5,2,2)
         quant(4,0,4)
         multiply(2)
         multiply(3)
         lift(5,0,2, "S")
         lift(5,2,2, "S")
-        quantise_x([1])
         turn(6,0,2); turn(6,2,2)
         quant(5,0,4)
         lift(6,0,2, "S")

@@ -69,26 +69,17 @@ def tile_caps_bn_s_kernel(tc, x, weight, bias, out):
             )
 
         load_x(0)
-        load_w(0, 0, 2)
-        load_w(0, 2, 2)
-        load_w(1, 0, 2)
-        load_w(1, 2, 2)
-        load_w(2, 0, 2)
-        load_w(2, 2, 2)
+        load_w(0, 0, O_TILES)
+        load_w(1, 0, O_TILES)
+        load_w(2, 0, O_TILES)
         load_bias()
-        load_w(3, 0, 2)
-        load_w(3, 2, 2)
+        load_w(3, 0, O_TILES)
         load_x(1)
-        load_w(4, 0, 2)
-        load_w(4, 2, 2)
-        load_w(5, 0, 2)
-        load_w(5, 2, 2)
-        load_w(6, 0, 2)
-        load_w(6, 2, 2)
-        load_w(7, 0, 1)
-        load_w(7, 1, 1)
-        load_w(7, 2, 1)
-        load_w(7, 3, 1)
+        load_w(4, 0, O_TILES)
+        load_w(5, 0, O_TILES)
+        load_w(6, 0, O_TILES)
+        load_w(7, 0, 2)
+        load_w(7, 2, 2)
 
         ident = consts.tile([P, P], F32)
         make_identity(nc, ident[:])

from contextlib import ExitStack

import concourse.mybir as mybir
from concourse.masks import make_identity

F32 = mybir.dt.float32
BF16 = mybir.dt.bfloat16
U32 = mybir.dt.uint32
U8 = mybir.dt.uint8
I32 = mybir.dt.int32
FP8X4 = mybir.dt.float8_e4m3fn_x4
ALU = mybir.AluOpType
ACT = mybir.ActivationFunctionType
AXIS = mybir.AxisListType

P = 128
PACK = 4
BATCH = 2
CAPS = 8
D = 512
HW = 16
EPS = 1e-5
SAMPLES = BATCH * HW
O_TILES = D // P
PAIR = 2
PAIRS = CAPS // PAIR
GROUPS = 2
GROUP_CAPS = CAPS // GROUPS
GROUP_CH = GROUP_CAPS * PACK

FLOPS = 2 * CAPS * D * D * SAMPLES


def tile_caps_bn_s_kernel(tc, x, weight, bias, out):
    nc = tc.nc
    with ExitStack() as ctx:
        consts = ctx.enter_context(tc.tile_pool(name="consts", bufs=1))
        acts = ctx.enter_context(tc.tile_pool(name="acts", bufs=GROUPS))
        caps = ctx.enter_context(tc.tile_pool(name="caps", bufs=CAPS))
        banks = ctx.enter_context(tc.psum_pool(name="banks", bufs=8))
        ctx.enter_context(tc.manual_schedule())

        bias_rows = consts.tile([P, D], BF16)
        nc.vector.memset(bias_rows[:].bitcast(I32), 0)
        x_view = x.rearrange("n (c q t) h w -> q n c (t h w)", c=CAPS, q=P, t=PACK)
        x_groups = []
        w_rows_all = []

        def load_x(g):
            x_group = acts.tile([P, BATCH, GROUP_CAPS, PACK, HW], BF16, name="x_group")
            for n in range(BATCH):
                nc.sync.dma_start(
                    out=x_group[:, n].rearrange("q c t s -> q c (t s)"),
                    in_=x_view[:, n, g * GROUP_CAPS : (g + 1) * GROUP_CAPS],
                )
            x_groups.append(x_group)

        def load_bias():
            nc.sync.dma_start(
                out=bias_rows[0:CAPS, :], in_=bias.rearrange("(c o) -> c o", c=CAPS)
            )

        def load_w(c, j0, tiles):
            if j0 == 0:
                w_rows_all.append(caps.tile([P, O_TILES, D], BF16, name="w_rows"))
            w_view = weight[c].rearrange("(p j) i -> p j i", j=O_TILES)
            nc.sync.dma_start(
                out=w_rows_all[c][:, j0 : j0 + tiles], in_=w_view[:, j0 : j0 + tiles]
            )

        load_x(0)
        load_w(0, 0, O_TILES)
        load_w(1, 0, O_TILES)
        load_w(2, 0, O_TILES)
        load_bias()
        load_w(3, 0, O_TILES)
        load_x(1)
        load_w(4, 0, O_TILES)
        load_w(5, 0, O_TILES)
        load_w(6, 0, O_TILES)
        load_w(7, 0, 2)
        load_w(7, 2, 2)

        ident = consts.tile([P, P], F32)
        make_identity(nc, ident[:])
        ones = consts.tile([P, 1], F32)
        nc.vector.memset(ones[:], 1.0)
        table_warmer = consts.tile([P, 1], F32)
        nc.scalar.activation(out=table_warmer[:], in_=ones[:], func=ACT.Abs_reciprocal_sqrt)
        eps = consts.tile([P, 1], F32)
        nc.vector.tensor_scalar_mul(out=eps[:], in0=ones[:], scalar1=EPS)

        grouped_all = {}
        turned_all = {}
        w_codes_all = {}
        w_scales_all = {}

        def turn(c, j0, tiles):
            w_words = w_rows_all[c][:].bitcast(F32)
            turned = banks.tile([P, tiles, 2, P], F32, name="bank")
            for jj in range(tiles):
                for u in range(2):
                    nc.tensor.transpose(
                        turned[:, jj, u, :], w_words[:, j0 + jj, u : 2 * P : 2], ident[:]
                    )
            turned_all[c, j0] = turned

        def lift(c, j0, tiles, engine):
            if c not in grouped_all:
                grouped_all[c] = caps.tile(
                    [P, O_TILES, P, PACK], BF16, align_bytes=64, name="grouped"
                )
            dst = grouped_all[c][:].bitcast(F32)[:, j0 : j0 + tiles]
            src = turned_all[c, j0][:].rearrange("q j u r -> q j r u")
            if engine == "S":
                nc.scalar.copy(out=dst, in_=src)
            else:
                nc.vector.tensor_copy(out=dst, in_=src)

        def quant(c, j0, tiles):
            if c not in w_codes_all:
                w_codes_all[c] = caps.tile([P, D], U32, align_bytes=64, name="w_codes")
                w_scales_all[c] = caps.tile([P, D], U8, align_bytes=64, name="w_scales")
            cols = slice(j0 * P, (j0 + tiles) * P)
            nc.vector.quantize_mx(
                out=w_codes_all[c][:, cols].bitcast(FP8X4),
                scales=w_scales_all[c][:, cols],
                in_=grouped_all[c][:, j0 : j0 + tiles].rearrange("q j r t -> q (j r t)"),
            )

        stats = consts.tile([P, CAPS * PACK // 2, 2, 3], F32)
        stat_of = stats[:].rearrange("q k e m -> q (k e) m")
        rstd = consts.tile([P, GROUPS * GROUP_CH], F32)
        centred = []
        xn = consts.tile([P, CAPS, SAMPLES, PACK], BF16, align_bytes=64)
        x_codes = consts.tile([P, CAPS * SAMPLES], U32, align_bytes=64)
        x_scales = consts.tile([P, CAPS * SAMPLES], U8, align_bytes=64)

        def chans(g):
            return slice(g * GROUP_CH, (g + 1) * GROUP_CH)

        def by_channel(g):
            return x_groups[g][:].rearrange("q n c t s -> q (c t) n s")

        def bn(g):
            for k in range(g * GROUP_CH // 2, (g + 1) * GROUP_CH // 2):
                c, e = divmod(k - g * GROUP_CH // 2, PACK // 2)
                nc.vector.bn_stats(
                    out=stats[:, k].rearrange("q e m -> q (e m)"),
                    in_=x_groups[g][:, :, c, 2 * e : 2 * e + 2, :].rearrange("q n t s -> q n s t"),
                )

        def centre(g, engine):
            t = acts.tile([P, GROUP_CH, BATCH, HW], F32, name="centred")
            engine.tensor_tensor(
                out=t[:],
                in0=by_channel(g),
                in1=stat_of[:, chans(g), 1]
                .unsqueeze(2)
                .unsqueeze(3)
                .to_broadcast([P, GROUP_CH, BATCH, HW]),
                op=ALU.subtract,
            )
            centred.append(t)

        def of(gs):
            return slice(gs[0] * GROUP_CH, (gs[-1] + 1) * GROUP_CH)

        def roots(gs=(0, 1)):
            nc.scalar.activation(
                out=rstd[:, of(gs)],
                in_=stat_of[:, of(gs), 2],
                func=ACT.Abs_reciprocal_sqrt,
                scale=1.0 / SAMPLES,
                bias=eps[:],
            )

        def normalise(g, engine):
            engine.tensor_tensor(
                out=xn[:, g * GROUP_CAPS : (g + 1) * GROUP_CAPS],
                in0=centred[g][:].rearrange("q (c t) n s -> q c (n s) t", t=PACK),
                in1=rstd[:, chans(g)]
                .rearrange("q (c t) -> q c t", t=PACK)
                .unsqueeze(2)
                .to_broadcast([P, GROUP_CAPS, SAMPLES, PACK]),
                op=ALU.mult,
            )

        def quantise_x(gs=(0, 1)):
            c0, c1 = gs[0] * GROUP_CAPS, (gs[-1] + 1) * GROUP_CAPS
            cols = slice(c0 * SAMPLES, c1 * SAMPLES)
            nc.vector.quantize_mx(
                out=x_codes[:, cols].bitcast(FP8X4),
                scales=x_scales[:, cols],
                in_=xn[:, c0:c1].rearrange("q c m t -> q (c m t)"),
            )

        out_view = out.rearrange("n (c p j) h w -> p c n (j h w)", c=CAPS, p=P, j=O_TILES)
        products = {}

        def multiply(c):
            h = c // GROUP_CAPS
            products[c] = banks.tile([P, O_TILES, GROUP_CAPS * SAMPLES], F32, name="bank")
            cols = slice(h * GROUP_CAPS * SAMPLES, (h + 1) * GROUP_CAPS * SAMPLES)
            for j in range(O_TILES):
                nc.tensor.matmul_mx(
                    out=products[c][:, j, :],
                    lhsT=w_codes_all[c][:, j * P : (j + 1) * P].bitcast(FP8X4),
                    lhsT_scale=w_scales_all[c][:, j * P : (j + 1) * P],
                    rhs=x_codes[:, cols].bitcast(FP8X4),
                    rhs_scale=x_scales[:, cols],
                    start=True,
                    stop=True,
                )

        def finish(c):
            k = c % GROUP_CAPS
            result = caps.tile([P, BATCH, O_TILES, HW], F32, name="result")
            nc.vector.tensor_tensor(
                out=result[:],
                in0=products[c][:, :, k * SAMPLES : (k + 1) * SAMPLES].rearrange(
                    "p j (n s) -> p n j s", n=BATCH
                ),
                in1=bias_sb[:, c, :].unsqueeze(1).unsqueeze(3).to_broadcast(
                    [P, BATCH, O_TILES, HW]
                ),
                op=ALU.add,
            )
            nc.sync.dma_start(
                out=out_view[:, c], in_=result[:].rearrange("p n j s -> p n (j s)")
            )

        def bias_turn():
            bias_words = bias_rows[:].bitcast(F32).rearrange("c (p v) -> c v p", v=2)
            bias_turned = banks.tile([P, 2, P], F32, name="bank")
            for v in range(2):
                nc.tensor.transpose(bias_turned[:, v, :], bias_words[:, v, :], ident[:])
            turned_all["bias"] = bias_turned

        bias_sb = consts.tile([P, CAPS, O_TILES], F32)

        def biascopy():
            nc.scalar.copy(
                out=bias_sb[:].rearrange("p c (v e) -> p c v e", v=2),
                in_=turned_all["bias"][:].bitcast(BF16).rearrange(
                    "p v (c e) -> p c v e", e=2
                )[:, 0:CAPS],
            )

        bn(0)
        centre(0, nc.vector)
        turn(0,0,2)
        roots([0])
        lift(0,0,2, "S")
        turn(0,2,2)
        lift(0,2,2, "S")
        normalise(0, nc.vector)
        turn(1,0,2); turn(1,2,2)
        quantise_x([0])
        lift(1,0,2, "S")
        quant(0,0,4)
        lift(1,2,2, "S")
        turn(2,0,2); turn(2,2,2)
        quant(1,0,4)
        lift(2,0,2, "S")
        lift(2,2,2, "S")
        turn(3,0,2); turn(3,2,2)
        bn(1)
        centre(1, nc.vector)
        quant(2,0,4)
        bias_turn()
        multiply(0)
        multiply(1)
        lift(3,0,2, "S")
        roots([1])
        lift(3,2,2, "S")
        biascopy()
        normalise(1, nc.vector)
        turn(4,0,2); turn(4,2,2)
        quant(3,0,4)
        lift(4,0,2, "S")
        lift(4,2,2, "S")
        finish(0)
        finish(1)
        quantise_x([1])
        turn(5,0,2); turn(5,2,2)
        quant(4,0,4)
        multiply(2)
        multiply(3)
        lift(5,0,2, "S")
        lift(5,2,2, "S")
        turn(6,0,2); turn(6,2,2)
        quant(5,0,4)
        lift(6,0,2, "S")
        lift(6,2,2, "S")
        finish(2)
        finish(3)
        turn(7,0,1); turn(7,1,1)
        turn(7,2,1); turn(7,3,1)
        quant(6,0,4)
        multiply(4)
        multiply(5)
        multiply(6)
        lift(7,0,1, "S")
        lift(7,1,1, "S")
        quant(7,0,2)
        lift(7,2,1, "S")
        lift(7,3,1, "S")
        finish(4)
        quant(7,2,2)
        multiply(7)
        finish(5)
        finish(6)
        finish(7)
